import numpy as np
import ml_dtypes


def mxq(x, axis, fmt="e4m3"):
    dtype, down = {"e4m3": (ml_dtypes.float8_e4m3fn, 7), "e5m2": (ml_dtypes.float8_e5m2, 14)}[fmt]
    v = np.moveaxis(np.asarray(x, np.float32).astype(ml_dtypes.bfloat16).astype(np.float64), axis, -1)
    blocks = v.reshape(v.shape[:-1] + (-1, 32))
    amax = np.abs(blocks).max(-1, keepdims=True)
    byte = np.maximum(np.where(amax > 0, np.frexp(amax)[1] - 1 + 127, 0) - down, 1)
    scale = np.exp2(byte - 127.0)
    codes = (blocks / scale).astype(np.float32).astype(dtype).astype(np.float64)
    return np.moveaxis((codes * scale).reshape(v.shape), -1, axis)


WIDE = False


def mx_kscale(k):
    if not WIDE:
        return np.ones(k)
    levels = np.array([30, -30])
    if k % 512:
        return np.exp2(np.random.permutation(np.resize(levels, k // 32))).repeat(32)
    a = np.empty((k // 512, 16))
    for p in range(k // 512):
        a[p, :8] = np.random.permutation(np.resize(levels, 8))
        for g in range(8):
            far = levels[np.abs(levels - a[p, g]) >= 10]
            a[p, g + 8] = far[np.random.randint(len(far))]
    return np.exp2(a.ravel()).repeat(32)


BF16 = ml_dtypes.bfloat16


def bf(x):
    return np.asarray(x, np.float32).astype(BF16)


def f64(x):
    return np.asarray(x).astype(np.float64)


H, I, B = 1024, 1024, 512


def sigmoid(v):
    return 1.0 / (1.0 + np.exp(-v))


def log_sigmoid(v):
    return np.minimum(v, 0.0) - np.log(1.0 + np.exp(-np.abs(v)))


def setup_inputs():
    s, t = mx_kscale(I), mx_kscale(H)

    def w():
        return bf(np.random.standard_normal((H, I)) * 0.7 / np.sqrt(I) / s)

    def r():
        return bf(np.random.standard_normal((H, H)) * 0.7 / np.sqrt(H) / t)

    def b():
        return bf(np.random.standard_normal(H) * 0.3)

    return {"x": bf(np.random.standard_normal((I, B)) * s[:, None]),
            "h_prev": bf(np.random.standard_normal((H, B)) * t[:, None]),
            "c_prev": bf(np.random.standard_normal((H, B))),
            "n_prev": bf(np.random.uniform(size=(H, B))),
            "m_prev": bf(np.random.standard_normal((H, B))),
            "w_input": w(), "w_forget": w(), "w_output": w(), "w_z": w(),
            "r_input": r(), "r_forget": r(), "r_output": r(), "r_z": r(),
            "b_input": b(), "b_forget": b(), "b_output": b(), "b_z": b()}


def reference(x, h_prev, c_prev, n_prev, m_prev,
              w_input, w_forget, w_output, w_z,
              r_input, r_forget, r_output, r_z,
              b_input, b_forget, b_output, b_z):
    xq = mxq(f64(x), 0, "e5m2")
    hq = mxq(f64(h_prev), 0, "e5m2")
    input_wave = (mxq(f64(w_input), 1, "e5m2") @ xq) + (mxq(f64(r_input), 1, "e5m2") @ hq) + f64(b_input)[:, None]
    forget_wave = (mxq(f64(w_forget), 1, "e5m2") @ xq) + (mxq(f64(r_forget), 1, "e5m2") @ hq) + f64(b_forget)[:, None]
    output_wave = (mxq(f64(w_output), 1, "e5m2") @ xq) + (mxq(f64(r_output), 1, "e5m2") @ hq) + f64(b_output)[:, None]
    z_wave = (mxq(f64(w_z), 1, "e5m2") @ xq) + (mxq(f64(r_z), 1, "e5m2") @ hq) + f64(b_z)[:, None]

    log_i = input_wave
    log_f = log_sigmoid(forget_wave)
    m_t = np.maximum(log_f + f64(m_prev), log_i)
    input_prime = np.exp(log_i - m_t)
    forget_prime = np.exp(log_f + f64(m_prev) - m_t)

    c_t = forget_prime * f64(c_prev) + input_prime * np.tanh(z_wave)
    n_t = forget_prime * f64(n_prev) + forget_prime
    h_wave = c_t / n_t
    h_t = sigmoid(output_wave) * np.tanh(h_wave)
    return (h_t, c_t, n_t, m_t)

@@ -1,0 +1,346 @@
+from contextlib import ExitStack
+
+import concourse.mybir as mybir
+from concourse.masks import make_identity
+
+H, K, B = 1024, 1024, 512
+FLOPS = 8 * 2 * H * K * B
+
+F32 = mybir.dt.float32
+BF16 = mybir.dt.bfloat16
+U32 = mybir.dt.uint32
+U8 = mybir.dt.uint8
+E5M2X4 = mybir.dt.float8_e5m2_x4
+ALU = mybir.AluOpType
+ACT = mybir.ActivationFunctionType
+
+P = 128
+PACK = 4
+K_PASS = P * PACK
+PASSES = K // K_PASS
+TILES = H // P
+FORGET, INPUT, Z, OUTPUT = range(4)
+STEPS = 4 * TILES
+W_BUFS = 14
+EXP_CAP = 80.0
+SPLIT = 192
+FIRST = 5
+VB1 = (0, 3, 5, 7)
+S_G = 4
+S_U = 11
+S_E = 12
+S_NS = 16
+S_N = 17
+S_T = 18
+S_M = 18
+S_R = 24
+S_C = 25
+S_CG = 6
+E_CG = 1
+LEAD = 3
+QL = 1
+VB1 = (6, 7)
+
+
+def tile_slstmcell_pa_kernel(tc, x, h_prev, c_prev, n_prev, m_prev,
+                                         w_input, w_forget, w_output, w_z,
+                                         r_input, r_forget, r_output, r_z,
+                                         b_input, b_forget, b_output, b_z,
+                                         out_h, out_c, out_n, out_m):
+    nc = tc.nc
+    by_tile = lambda t: t.rearrange("(p j) c -> p j c", j=TILES)
+    weights = [(by_tile(w), by_tile(r)) for w, r in
+               ((w_forget, r_forget), (w_input, r_input), (w_z, r_z), (w_output, r_output))]
+    biases = (b_forget, b_input, b_z, b_output)
+    acts = (x, h_prev)
+    out_h, out_c, out_n, out_m = by_tile(out_h), by_tile(out_c), by_tile(out_n), by_tile(out_m)
+
+    with ExitStack() as ctx:
+        keep = ctx.enter_context(tc.tile_pool(name="keep", bufs=1))
+        stream = ctx.enter_context(tc.tile_pool(name="stream", bufs=2))
+        psum = ctx.enter_context(tc.psum_pool(name="psum", bufs=4))
+        ctx.enter_context(tc.manual_schedule())
+
+        ident = keep.tile([P, P], F32, name="ident")
+        bias_raw = keep.tile([P, 4, 2 * TILES], BF16, name="bias_raw")
+        bias = keep.tile([P, 4, TILES], F32, name="bias")
+        neg_bias_f = keep.tile([P, TILES], F32, name="neg_bias_f")
+        c_sb = keep.tile([P, TILES, B], BF16, name="c_sb")
+        nm_sb = keep.tile([P, 2, TILES, B], BF16, name="nm_sb")
+        n_sb, m_sb = nm_sb[:, 0, :, :], nm_sb[:, 1, :, :]
+        lane_e = nm_sb[:].rearrange("p s j b -> p (s j b)").bitcast(F32).rearrange("p (j b) -> p j b", b=B)
+        act_codes = keep.tile([P, 2 * PASSES, B], U32, name="act_codes", align_bytes=64)
+        act_scales = keep.tile([P, 2 * PASSES, B], U8, name="act_scales", align_bytes=64)
+        lane_t = keep.tile([P, TILES, B], F32, name="lane_t")
+        lane_m = keep.tile([P, TILES, B], F32, name="lane_m")
+        lane_n = keep.tile([P, TILES, B], F32, name="lane_n")
+        lane_g = keep.tile([P, TILES, B], F32, name="lane_g")
+        lane_r = keep.tile([P, TILES, B], F32, name="lane_r")
+
+        w_raw, banks, w_grouped, w_mx, waves, act_raw, act_grouped, tanh_z, sig_o = {}, {}, {}, {}, {}, {}, {}, {}, {}
+        done_h = set()
+
+        def load_weight(pair, side, tiles=(slice(0, 2),)):
+            gate, j0 = divmod(2 * pair, TILES)
+            if (pair, side) not in w_raw:
+                w_raw[pair, side] = stream.tile([P, 2, K], BF16, name="raw", bufs=W_BUFS)
+            for s in tiles:
+                nc.sync.dma_start(out=w_raw[pair, side][:, s, :], in_=weights[gate][side][:, j0 + s.start:j0 + s.stop, :])
+
+        def load_act(a):
+            side, g = divmod(a, PASSES)
+            act_raw[a] = stream.tile([P, PACK, B], BF16, name="raw", bufs=W_BUFS)
+            nc.sync.dma_start(out=act_raw[a][:], in_=acts[side][g * K_PASS:(g + 1) * K_PASS, :].rearrange("(p t) b -> p t b", t=PACK))
+
+        def group_act(a, copy, cols):
+            if a not in act_grouped:
+                act_grouped[a] = stream.tile([P, B, PACK], BF16, name="grouped", bufs=4, align_bytes=64)
+            copy(out=act_grouped[a][:, cols, :], in_=act_raw[a][:, :, cols].rearrange("p t b -> p b t"))
+
+        def quantise_act(a):
+            nc.vector.quantize_mx(out=act_codes[:, a, :].bitcast(E5M2X4), scales=act_scales[:, a, :],
+                                  in_=act_grouped[a][:].rearrange("p b t -> p (b t)"))
+
+        def transpose_weights(step, side):
+            words = w_raw[step // 2, side][:, step % 2, :].bitcast(F32)
+            bank = psum.tile([P, PASSES, 2, P], F32, name="turned")
+            banks[step, side] = bank
+            for g in range(PASSES):
+                for u in range(2):
+                    nc.tensor.transpose(bank[:, g, u, :], words[:, 2 * P * g + u:2 * P * (g + 1):2], ident[:])
+
+        def empty_bank(step, side, copy):
+            if step not in w_grouped:
+                w_grouped[step] = stream.tile([P, 2, PASSES * P * PACK], BF16, name="grouped", bufs=4, align_bytes=64)
+            dst = w_grouped[step][:, side, :].bitcast(F32).rearrange("p (g r u) -> p g r u", g=PASSES, u=2)
+            copy(out=dst, in_=banks[step, side][:].rearrange("p g u r -> p g r u"))
+
+        def quantise_weights(step):
+            codes = stream.tile([P, 2 * PASSES * P], U32, name="w_codes", bufs=4, align_bytes=64)
+            scales = stream.tile([P, 2 * PASSES * P], U8, name="w_scales", bufs=4, align_bytes=64)
+            w_mx[step] = codes, scales
+            nc.vector.quantize_mx(out=codes[:].bitcast(E5M2X4), scales=scales[:],
+                                  in_=w_grouped[step][:].rearrange("p s c -> p (s c)"))
+
+        def multiply(step):
+            codes, scales = w_mx[step]
+            wave = psum.tile([P, B], F32, name="wave")
+            waves[step] = wave
+            for a in range(2 * PASSES):
+                cols = slice(a * P, (a + 1) * P)
+                nc.tensor.matmul_mx(out=wave[:], lhsT=codes[:, cols].bitcast(E5M2X4), lhsT_scale=scales[:, cols],
+                                    rhs=act_codes[:, a, :].bitcast(E5M2X4), rhs_scale=act_scales[:, a, :],
+                                    start=(a == 0), stop=(a == 2 * PASSES - 1))
+
+        def col(gate, j):
+            return bias[:, gate, j:j + 1]
+
+        def act(out, in_, func, **kw):
+            nc.scalar.activation(out=out, in_=in_, func=func, **kw)
+
+        def stt(out, in0, scalar, op0, op1, in1):
+            nc.vector.scalar_tensor_tensor(out=out, in0=in0, scalar=scalar, in1=in1, op0=op0, op1=op1)
+
+        def tt(out, in0, op, in1):
+            nc.vector.tensor_tensor(out=out, in0=in0, in1=in1, op=op)
+
+        def abs_f(j):
+            act(lane_t[:, j, :], waves[j][:], ACT.Abs, bias=col(FORGET, j))
+
+        def min_f(j):
+            stt(lane_m[:, j, :], waves[j][:], neg_bias_f[:, j:j + 1], ALU.min, ALU.add, m_sb[:, j, :])
+
+        def log_n(js):
+            act(lane_n[:, js, :], n_sb[:, js, :], ACT.Ln, bias=1.0)
+
+        def exp_f(js):
+            act(lane_t[:, js, :], lane_t[:, js, :], ACT.Exp, scale=-1.0)
+
+        def log_f(js):
+            act(lane_t[:, js, :], lane_t[:, js, :], ACT.Ln, bias=1.0)
+
+        def inv_n(js):
+            act(lane_r[:, js, :], lane_n[:, js, :], ACT.Exp, scale=-1.0)
+
+        def c_over_n(js):
+            tt(lane_r[:, js, :], lane_r[:, js, :], ALU.mult, c_sb[:, js, :])
+
+        def carry(j):
+            stt(lane_m[:, j, :], lane_m[:, j, :], col(FORGET, j), ALU.add, ALU.subtract, lane_t[:, j, :])
+
+        def gap(j):
+            stt(lane_t[:, j, :], waves[TILES + j][:], col(INPUT, j), ALU.add, ALU.subtract, lane_m[:, j, :])
+
+        def new_m(j):
+            stt(lane_m[:, j, :], lane_t[:, j, :], 0.0, ALU.max, ALU.add, lane_m[:, j, :])
+
+        def log_gain(j):
+            stt(lane_g[:, j, :], lane_t[:, j, :], EXP_CAP, ALU.min, ALU.subtract, lane_n[:, j, :])
+
+        def log_new_n(j):
+            stt(lane_n[:, j, :], lane_g[:, j, :], -1.0, ALU.mult, ALU.min, lane_n[:, j, :])
+
+        def gain(j):
+            act(lane_e[:, j, :], lane_g[:, j, :], ACT.Exp)
+
+        def new_n(j):
+            act(lane_n[:, j, :], lane_n[:, j, :], ACT.Exp)
+
+        def tanh_wave(j):
+            tanh_z[j] = stream.tile([P, B], F32, name="tanh_z", bufs=3)
+            act(tanh_z[j][:], waves[2 * TILES + j][:], ACT.Tanh, bias=col(Z, j))
+
+        def gained(j):
+            tt(lane_e[:, j, :], lane_e[:, j, :], ALU.mult, tanh_z[j][:])
+
+        def ratio(j):
+            tt(lane_r[:, j, :], lane_r[:, j, :], ALU.add, lane_e[:, j, :])
+
+        def new_c(j):
+            c_new = stream.tile([P, B], F32, name="c_new", bufs=3)
+            tt(c_new[:], lane_r[:, j, :], ALU.mult, lane_n[:, j, :])
+            nc.sync.dma_start(out=out_c[:, j, :], in_=c_new[:])
+
+        def tanh_ratio(j):
+            act(lane_t[:, j, :], lane_r[:, j, :], ACT.Tanh)
+
+        def sigmoid_wave(j):
+            sig_o[j] = stream.tile([P, B], F32, name="sig_o", bufs=3)
+            act(sig_o[j][:], waves[3 * TILES + j][:], ACT.Sigmoid, bias=col(OUTPUT, j))
+
+        def new_h(j):
+            tt(lane_t[:, j, :], lane_t[:, j, :], ALU.mult, sig_o[j][:])
+            nc.sync.dma_start(out=out_h[:, j, :], in_=lane_t[:, j, :])
+
+        def at(step, first, fn, count=TILES):
+            if first <= step < first + count:
+                fn(step - first)
+
+        def pair_at(step, first, fn, every=2):
+            q, rest = divmod(step - first, every)
+            if rest == 0 and 0 <= q < TILES // 2:
+                fn(slice(2 * q, 2 * q + 2))
+
+        on_scalar, on_vector = nc.scalar.copy, nc.vector.tensor_copy
+        one, two = slice(0, 1), slice(1, 2)
+
+        make_identity(nc, ident[:])
+
+        def load_state(dst, src, js):
+            nc.sync.dma_start(out=dst[:, js, :], in_=by_tile(src)[:, js, :])
+
+        def load_biases():
+            for gate in range(4):
+                nc.sync.dma_start(out=bias_raw[:, gate, 0:TILES], in_=biases[gate].rearrange("(p j) -> p j", j=TILES))
+
+        load_state(n_sb, n_prev, one)
+        load_act(0)
+        load_weight(0, 0, (one,))
+        load_act(1)
+        load_weight(0, 1, (one,))
+        load_act(2)
+        load_weight(0, 0, (two,))
+        load_act(3)
+        load_weight(0, 1, (two,))
+        load_weight(1, 0)
+        load_weight(1, 1)
+        load_biases()
+        load_state(n_sb, n_prev, slice(1, 4))
+        load_weight(2, 0)
+        load_weight(2, 1)
+        load_state(m_sb, m_prev, slice(0, 2))
+        load_state(n_sb, n_prev, slice(4, TILES))
+        load_weight(3, 0)
+        load_weight(3, 1)
+        load_state(m_sb, m_prev, slice(2, TILES))
+        load_state(c_sb, c_prev, slice(0, TILES))
+        for pair in range(4, FIRST):
+            load_weight(pair, 0)
+            load_weight(pair, 1)
+
+        left, right = slice(0, SPLIT), slice(SPLIT, B)
+        log_n(one)
+        group_act(0, on_scalar, left)
+        group_act(0, on_vector, right)
+        transpose_weights(0, 0)
+        empty_bank(0, 0, on_scalar)
+        quantise_act(0)
+        group_act(1, on_scalar, left)
+        group_act(1, on_vector, right)
+        transpose_weights(0, 1)
+        empty_bank(0, 1, on_scalar)
+        quantise_act(1)
+        group_act(2, on_scalar, left)
+        group_act(2, on_vector, right)
+        quantise_weights(0)
+        transpose_weights(1, 0)
+        empty_bank(1, 0, on_scalar)
+        quantise_act(2)
+        group_act(3, on_scalar, left)
+        group_act(3, on_vector, right)
+        transpose_weights(1, 1)
+        empty_bank(1, 1, on_scalar)
+        quantise_act(3)
+        transpose_weights(2, 0)
+        transpose_weights(2, 1)
+        empty_bank(2, 0, on_vector)
+        empty_bank(2, 1, on_vector)
+        nc.vector.tensor_copy(out=bias[:], in_=bias_raw[:, :, 0:TILES])
+        nc.vector.tensor_scalar(out=neg_bias_f[:], in0=bias[:, FORGET, :], scalar1=-1.0, scalar2=None, op0=ALU.mult)
+
+        single = lambda fn: (lambda j: fn(slice(j, j + 1)))
+        store_m = lambda js: nc.sync.dma_start(out=out_m[:, js, :], in_=lane_m[:, js, :])
+        store_n = lambda js: nc.sync.dma_start(out=out_n[:, js, :], in_=lane_n[:, js, :])
+
+        for step in range(STEPS + 1):
+            ahead = step + LEAD
+            prep = ahead < STEPS
+            if step % 2 == 0 and FIRST + step // 2 < STEPS // 2:
+                load_weight(FIRST + step // 2, 0)
+                load_weight(FIRST + step // 2, 1)
+            if prep:
+                transpose_weights(ahead, 0)
+                transpose_weights(ahead, 1)
+            if step < STEPS:
+                multiply(step)
+            vector_banks = (1 if step in VB1 else 2) if step < 10 else 0
+
+            at(step, 17, tanh_wave)
+            at(step, S_N, new_n)
+            at(step, 25, sigmoid_wave)
+            if step + QL < STEPS:
+                quantise_weights(step + QL)
+            at(step, 1, min_f)
+            if step == 0:
+                log_n(slice(1, 4))
+            if step == 1:
+                log_n(slice(4, TILES))
+            if step == 3:
+                exp_f(slice(0, 2))
+            at(step, 2, single(exp_f)) if 3 < step < 9 else None
+            at(step, 1, abs_f)
+            if step == 10:
+                carry(0)
+            at(step, 9, carry) if step > 9 else None
+            at(step, S_NS, log_new_n)
+            at(step, S_U, log_gain)
+            at(step, 10, gap)
+            at(step, S_T, gained)
+            at(step, S_M, new_m)
+            at(step, S_R, ratio)
+            at(step, 25, new_h)
+            if step == 8:
+                exp_f(slice(7, 8))
+            if step == 9:
+                log_f(slice(0, 2))
+            pair_at(step, 8, log_f, every=1) if step > 8 else None
+            at(step, S_E, gain)
+            if prep:
+                for side in range(2):
+                    empty_bank(ahead, side, on_vector if side < vector_banks else on_scalar)
+            pair_at(step, S_G, inv_n, every=1)
+            pair_at(step, S_CG, c_over_n, every=E_CG)
+            at(step, S_R, tanh_ratio)
+            at(step, S_C, new_c)
+            pair_at(step, S_M + 2, store_m)
+            pair_at(step, S_N + 2, store_n)

@@ -19,27 +19,32 @@ PACK = 4
 K_PASS = P * PACK
 PASSES = K // K_PASS
 TILES = H // P
+PAIRS = TILES // 2
 FORGET, INPUT, Z, OUTPUT = range(4)
-STEPS = 4 * TILES
-W_BUFS = 14
+ROUNDS = 4 * PAIRS
+RAW_BUFS = 12
 EXP_CAP = 80.0
+ON_POOL = True
+LT = 3
 SPLIT = 192
-FIRST = 5
-VB1 = (0, 3, 5, 7)
-S_G = 4
-S_U = 11
-S_E = 12
-S_NS = 16
-S_N = 17
-S_T = 18
-S_M = 18
+FIRST = 4
+VB = (0, 1, 2, 2, 2, 2, 2, 2, 2, 2)
+Q_ODD = 1
+S_D = 11
+S_L = (9, 10, 11)
+S_F = 13
+S_E = 17
+S_T = 19
+S_W = 20
 S_R = 24
-S_C = 25
-S_CG = 6
-E_CG = 1
-LEAD = 3
-QL = 1
-VB1 = (6, 7)
+S_N = 16
+S_C = 24
+S_H = 26
+S_G = (3, 4, 5, 14)
+Q_EARLY = 99
+HV = 0
+RUN = 2
+VB = (0, 2, 2, 2, 2, 2, 2, 2, 2, 2)
 
 
 def tile_slstmcell_pa_kernel(tc, x, h_prev, c_prev, n_prev, m_prev,
@@ -66,69 +71,80 @@ def tile_slstmcell_pa_kernel(tc, x, h_prev, c_prev, n_prev, m_prev,
         bias = keep.tile([P, 4, TILES], F32, name="bias")
         neg_bias_f = keep.tile([P, TILES], F32, name="neg_bias_f")
         c_sb = keep.tile([P, TILES, B], BF16, name="c_sb")
-        nm_sb = keep.tile([P, 2, TILES, B], BF16, name="nm_sb")
-        n_sb, m_sb = nm_sb[:, 0, :, :], nm_sb[:, 1, :, :]
-        lane_e = nm_sb[:].rearrange("p s j b -> p (s j b)").bitcast(F32).rearrange("p (j b) -> p j b", b=B)
+        n_sb = keep.tile([P, TILES, B], BF16, name="n_sb")
+        m_sb = keep.tile([P, TILES, B], BF16, name="m_sb")
         act_codes = keep.tile([P, 2 * PASSES, B], U32, name="act_codes", align_bytes=64)
         act_scales = keep.tile([P, 2 * PASSES, B], U8, name="act_scales", align_bytes=64)
         lane_t = keep.tile([P, TILES, B], F32, name="lane_t")
         lane_m = keep.tile([P, TILES, B], F32, name="lane_m")
         lane_n = keep.tile([P, TILES, B], F32, name="lane_n")
-        lane_g = keep.tile([P, TILES, B], F32, name="lane_g")
+        lane_1 = keep.tile([P, TILES, B], F32, name="lane_1")
         lane_r = keep.tile([P, TILES, B], F32, name="lane_r")
 
         w_raw, banks, w_grouped, w_mx, waves, act_raw, act_grouped, tanh_z, sig_o = {}, {}, {}, {}, {}, {}, {}, {}, {}
-        done_h = set()
+        pair = lambda k: slice(2 * k, 2 * k + 2)
 
-        def load_weight(pair, side, tiles=(slice(0, 2),)):
-            gate, j0 = divmod(2 * pair, TILES)
-            if (pair, side) not in w_raw:
-                w_raw[pair, side] = stream.tile([P, 2, K], BF16, name="raw", bufs=W_BUFS)
-            for s in tiles:
-                nc.sync.dma_start(out=w_raw[pair, side][:, s, :], in_=weights[gate][side][:, j0 + s.start:j0 + s.stop, :])
+        def load_weight(rnd, side, s=slice(0, 2)):
+            gate, j0 = divmod(2 * rnd, TILES)
+            if (rnd, side) not in w_raw:
+                w_raw[rnd, side] = stream.tile([P, 2, K], BF16, name="raw", bufs=RAW_BUFS)
+            nc.sync.dma_start(out=w_raw[rnd, side][:, s, :], in_=weights[gate][side][:, j0 + s.start:j0 + s.stop, :])
 
         def load_act(a):
             side, g = divmod(a, PASSES)
-            act_raw[a] = stream.tile([P, PACK, B], BF16, name="raw", bufs=W_BUFS)
+            act_raw[a] = stream.tile([P, PACK, B], BF16, name="raw", bufs=RAW_BUFS)
             nc.sync.dma_start(out=act_raw[a][:], in_=acts[side][g * K_PASS:(g + 1) * K_PASS, :].rearrange("(p t) b -> p t b", t=PACK))
+
+        def load_state(dst, src, js):
+            nc.sync.dma_start(out=dst[:, js, :], in_=by_tile(src)[:, js, :])
+
+        def load_biases():
+            for gate in range(4):
+                nc.sync.dma_start(out=bias_raw[:, gate, 0:TILES], in_=biases[gate].rearrange("(p j) -> p j", j=TILES))
 
         def group_act(a, copy, cols):
             if a not in act_grouped:
-                act_grouped[a] = stream.tile([P, B, PACK], BF16, name="grouped", bufs=4, align_bytes=64)
-            copy(out=act_grouped[a][:, cols, :], in_=act_raw[a][:, :, cols].rearrange("p t b -> p b t"))
+                act_grouped[a] = stream.tile([P, B, PACK], BF16, name="act_grouped", bufs=3, align_bytes=64)
+            copy(out=act_grouped[a][:, cols, :].rearrange("p (c i) t -> p c t i", i=4),
+                 in_=act_raw[a][:, :, cols].rearrange("p t (c i) -> p c t i", i=4))
 
         def quantise_act(a):
             nc.vector.quantize_mx(out=act_codes[:, a, :].bitcast(E5M2X4), scales=act_scales[:, a, :],
                                   in_=act_grouped[a][:].rearrange("p b t -> p (b t)"))
 
-        def transpose_weights(step, side):
-            words = w_raw[step // 2, side][:, step % 2, :].bitcast(F32)
+        def transpose_weights(rnd, side, e):
+            words = w_raw[rnd, side][:, e, :].bitcast(F32)
             bank = psum.tile([P, PASSES, 2, P], F32, name="turned")
-            banks[step, side] = bank
+            banks[rnd, side, e] = bank
             for g in range(PASSES):
                 for u in range(2):
                     nc.tensor.transpose(bank[:, g, u, :], words[:, 2 * P * g + u:2 * P * (g + 1):2], ident[:])
 
-        def empty_bank(step, side, copy):
-            if step not in w_grouped:
-                w_grouped[step] = stream.tile([P, 2, PASSES * P * PACK], BF16, name="grouped", bufs=4, align_bytes=64)
-            dst = w_grouped[step][:, side, :].bitcast(F32).rearrange("p (g r u) -> p g r u", g=PASSES, u=2)
-            copy(out=dst, in_=banks[step, side][:].rearrange("p g u r -> p g r u"))
+        def empty_bank(rnd, side, e, copy):
+            if rnd not in w_grouped:
+                w_grouped[rnd] = stream.tile([P, 2, 2, PASSES * P * PACK], BF16, name="w_grouped", bufs=3, align_bytes=64)
+            dst = w_grouped[rnd][:, side, e, :].bitcast(F32).rearrange("p (g r u) -> p g r u", g=PASSES, u=2)
+            copy(out=dst, in_=banks[rnd, side, e][:].rearrange("p g u r -> p g r u"))
 
-        def quantise_weights(step):
-            codes = stream.tile([P, 2 * PASSES * P], U32, name="w_codes", bufs=4, align_bytes=64)
-            scales = stream.tile([P, 2 * PASSES * P], U8, name="w_scales", bufs=4, align_bytes=64)
-            w_mx[step] = codes, scales
-            nc.vector.quantize_mx(out=codes[:].bitcast(E5M2X4), scales=scales[:],
-                                  in_=w_grouped[step][:].rearrange("p s c -> p (s c)"))
+        def quantise_weights(rnd, sides=slice(0, 2)):
+            if rnd not in w_mx:
+                codes = stream.tile([P, 2, 2 * PASSES * P], U32, name="w_codes", bufs=3, align_bytes=64)
+                scales = stream.tile([P, 2, 2 * PASSES * P], U8, name="w_scales", bufs=3, align_bytes=64)
+                w_mx[rnd] = codes, scales
+            codes, scales = w_mx[rnd]
+            nc.vector.quantize_mx(out=codes[:, sides, :].rearrange("p s c -> p (s c)").bitcast(E5M2X4),
+                                  scales=scales[:, sides, :].rearrange("p s c -> p (s c)"),
+                                  in_=w_grouped[rnd][:, sides, :, :].rearrange("p s e c -> p (s e c)"))
 
-        def multiply(step):
-            codes, scales = w_mx[step]
-            wave = psum.tile([P, B], F32, name="wave")
-            waves[step] = wave
-            for a in range(2 * PASSES):
-                cols = slice(a * P, (a + 1) * P)
-                nc.tensor.matmul_mx(out=wave[:], lhsT=codes[:, cols].bitcast(E5M2X4), lhsT_scale=scales[:, cols],
+        def multiply(rnd, e, side):
+            codes, scales = w_mx[rnd]
+            if side == 0:
+                waves[2 * rnd + e] = psum.tile([P, B], F32, name="wave")
+            for g in range(PASSES):
+                cols = slice((e * PASSES + g) * P, (e * PASSES + g + 1) * P)
+                a = side * PASSES + g
+                nc.tensor.matmul_mx(out=waves[2 * rnd + e][:],
+                                    lhsT=codes[:, side, cols].bitcast(E5M2X4), lhsT_scale=scales[:, side, cols],
                                     rhs=act_codes[:, a, :].bitcast(E5M2X4), rhs_scale=act_scales[:, a, :],
                                     start=(a == 0), stop=(a == 2 * PASSES - 1))
 
@@ -144,6 +160,8 @@ def tile_slstmcell_pa_kernel(tc, x, h_prev, c_prev, n_prev, m_prev,
         def tt(out, in0, op, in1):
             nc.vector.tensor_tensor(out=out, in0=in0, in1=in1, op=op)
 
+        clamp_engine = nc.gpsimd if ON_POOL else nc.vector
+
         def abs_f(j):
             act(lane_t[:, j, :], waves[j][:], ACT.Abs, bias=col(FORGET, j))
 
@@ -151,7 +169,7 @@ def tile_slstmcell_pa_kernel(tc, x, h_prev, c_prev, n_prev, m_prev,
             stt(lane_m[:, j, :], waves[j][:], neg_bias_f[:, j:j + 1], ALU.min, ALU.add, m_sb[:, j, :])
 
         def log_n(js):
-            act(lane_n[:, js, :], n_sb[:, js, :], ACT.Ln, bias=1.0)
+            act(lane_r[:, js, :], n_sb[:, js, :], ACT.Ln, bias=1.0)
 
         def exp_f(js):
             act(lane_t[:, js, :], lane_t[:, js, :], ACT.Exp, scale=-1.0)
@@ -160,10 +178,7 @@ def tile_slstmcell_pa_kernel(tc, x, h_prev, c_prev, n_prev, m_prev,
             act(lane_t[:, js, :], lane_t[:, js, :], ACT.Ln, bias=1.0)
 
         def inv_n(js):
-            act(lane_r[:, js, :], lane_n[:, js, :], ACT.Exp, scale=-1.0)
-
-        def c_over_n(js):
-            tt(lane_r[:, js, :], lane_r[:, js, :], ALU.mult, c_sb[:, js, :])
+            act(lane_r[:, js, :], lane_r[:, js, :], ACT.Exp, scale=-1.0)
 
         def carry(j):
             stt(lane_m[:, j, :], lane_m[:, j, :], col(FORGET, j), ALU.add, ALU.subtract, lane_t[:, j, :])
@@ -172,175 +187,205 @@ def tile_slstmcell_pa_kernel(tc, x, h_prev, c_prev, n_prev, m_prev,
             stt(lane_t[:, j, :], waves[TILES + j][:], col(INPUT, j), ALU.add, ALU.subtract, lane_m[:, j, :])
 
         def new_m(j):
-            stt(lane_m[:, j, :], lane_t[:, j, :], 0.0, ALU.max, ALU.add, lane_m[:, j, :])
+            stt(lane_m[:, j, :], waves[TILES + j][:], col(INPUT, j), ALU.add, ALU.max, lane_m[:, j, :])
 
-        def log_gain(j):
-            stt(lane_g[:, j, :], lane_t[:, j, :], EXP_CAP, ALU.min, ALU.subtract, lane_n[:, j, :])
+        def clamp_gap(js):
+            clamp_engine.tensor_scalar(out=lane_t[:, js, :], in0=lane_t[:, js, :], scalar1=EXP_CAP, scalar2=-EXP_CAP, op0=ALU.min, op1=ALU.max)
 
-        def log_new_n(j):
-            stt(lane_n[:, j, :], lane_g[:, j, :], -1.0, ALU.mult, ALU.min, lane_n[:, j, :])
+        def one_plus_n(js):
+            clamp_engine.tensor_scalar(out=lane_1[:, js, :], in0=n_sb[:, js, :], scalar1=1.0, scalar2=1.0, op0=ALU.add, op1=ALU.mult)
 
-        def gain(j):
-            act(lane_e[:, j, :], lane_g[:, j, :], ACT.Exp)
+        def gain(js):
+            act(lane_t[:, js, :], lane_t[:, js, :], ACT.Exp)
 
-        def new_n(j):
-            act(lane_n[:, j, :], lane_n[:, j, :], ACT.Exp)
+        def forget_prime(js):
+            act(lane_n[:, js, :], lane_t[:, js, :], ACT.Exp, scale=-1.0)
 
         def tanh_wave(j):
-            tanh_z[j] = stream.tile([P, B], F32, name="tanh_z", bufs=3)
-            act(tanh_z[j][:], waves[2 * TILES + j][:], ACT.Tanh, bias=col(Z, j))
+            if j % 2 == 0:
+                tanh_z[j // 2] = stream.tile([P, 2, B], F32, name="wave_sb", bufs=3)
+            act(tanh_z[j // 2][:, j % 2, :], waves[2 * TILES + j][:], ACT.Tanh, bias=col(Z, j))
 
-        def gained(j):
-            tt(lane_e[:, j, :], lane_e[:, j, :], ALU.mult, tanh_z[j][:])
+        def gained(k):
+            tt(lane_t[:, pair(k), :], lane_t[:, pair(k), :], ALU.mult, tanh_z[k][:])
 
-        def ratio(j):
-            tt(lane_r[:, j, :], lane_r[:, j, :], ALU.add, lane_e[:, j, :])
+        def cell(k):
+            tt(lane_t[:, pair(k), :], lane_t[:, pair(k), :], ALU.add, c_sb[:, pair(k), :])
 
-        def new_c(j):
-            c_new = stream.tile([P, B], F32, name="c_new", bufs=3)
-            tt(c_new[:], lane_r[:, j, :], ALU.mult, lane_n[:, j, :])
-            nc.sync.dma_start(out=out_c[:, j, :], in_=c_new[:])
+        def ratio(k):
+            tt(lane_r[:, pair(k), :], lane_r[:, pair(k), :], ALU.mult, lane_t[:, pair(k), :])
 
-        def tanh_ratio(j):
-            act(lane_t[:, j, :], lane_r[:, j, :], ACT.Tanh)
+        def new_c(k):
+            stt(lane_t[:, pair(k), :], lane_n[:, pair(k), :], 1.0, ALU.min, ALU.mult, lane_t[:, pair(k), :])
+            nc.sync.dma_start(out=out_c[:, pair(k), :], in_=lane_t[:, pair(k), :])
+
+        def new_n(k):
+            stt(lane_1[:, pair(k), :], lane_n[:, pair(k), :], 1.0, ALU.min, ALU.mult, lane_1[:, pair(k), :])
+            nc.sync.dma_start(out=out_n[:, pair(k), :], in_=lane_1[:, pair(k), :])
+
+        def store_m(k):
+            nc.sync.dma_start(out=out_m[:, pair(k), :], in_=lane_m[:, pair(k), :])
+
+        def tanh_ratio(k):
+            act(lane_r[:, pair(k), :], lane_r[:, pair(k), :], ACT.Tanh)
 
         def sigmoid_wave(j):
-            sig_o[j] = stream.tile([P, B], F32, name="sig_o", bufs=3)
-            act(sig_o[j][:], waves[3 * TILES + j][:], ACT.Sigmoid, bias=col(OUTPUT, j))
+            if j % 2 == 0:
+                sig_o[j // 2] = stream.tile([P, 2, B], F32, name="wave_sb", bufs=3)
+            act(sig_o[j // 2][:, j % 2, :], waves[3 * TILES + j][:], ACT.Sigmoid, bias=col(OUTPUT, j))
 
-        def new_h(j):
-            tt(lane_t[:, j, :], lane_t[:, j, :], ALU.mult, sig_o[j][:])
-            nc.sync.dma_start(out=out_h[:, j, :], in_=lane_t[:, j, :])
-
-        def at(step, first, fn, count=TILES):
-            if first <= step < first + count:
-                fn(step - first)
-
-        def pair_at(step, first, fn, every=2):
-            q, rest = divmod(step - first, every)
-            if rest == 0 and 0 <= q < TILES // 2:
-                fn(slice(2 * q, 2 * q + 2))
+        def new_h(js):
+            k = js.start // 2
+            tt(lane_r[:, js, :], lane_r[:, js, :], ALU.mult, sig_o[k][:, js.start - 2 * k:js.stop - 2 * k, :])
+            nc.sync.dma_start(out=out_h[:, js, :], in_=lane_r[:, js, :])
 
         on_scalar, on_vector = nc.scalar.copy, nc.vector.tensor_copy
         one, two = slice(0, 1), slice(1, 2)
+        left, right = slice(0, SPLIT), slice(SPLIT, B)
 
         make_identity(nc, ident[:])
-
-        def load_state(dst, src, js):
-            nc.sync.dma_start(out=dst[:, js, :], in_=by_tile(src)[:, js, :])
-
-        def load_biases():
-            for gate in range(4):
-                nc.sync.dma_start(out=bias_raw[:, gate, 0:TILES], in_=biases[gate].rearrange("(p j) -> p j", j=TILES))
-
         load_state(n_sb, n_prev, one)
         load_act(0)
-        load_weight(0, 0, (one,))
+        load_weight(0, 0, one)
         load_act(1)
-        load_weight(0, 1, (one,))
+        load_weight(0, 0, two)
         load_act(2)
-        load_weight(0, 0, (two,))
+        load_weight(0, 1, one)
         load_act(3)
-        load_weight(0, 1, (two,))
-        load_weight(1, 0)
-        load_weight(1, 1)
-        load_biases()
+        load_weight(0, 1, two)
+        load_weight(1, 0, one)
+        load_weight(1, 1, one)
+        load_weight(1, 0, two)
+        load_weight(1, 1, two)
         load_state(n_sb, n_prev, slice(1, 4))
-        load_weight(2, 0)
-        load_weight(2, 1)
-        load_state(m_sb, m_prev, slice(0, 2))
         load_state(n_sb, n_prev, slice(4, TILES))
-        load_weight(3, 0)
-        load_weight(3, 1)
+        load_biases()
+        load_weight(2, 0, one)
+        load_weight(2, 1, one)
+        load_state(m_sb, m_prev, pair(0))
+        load_weight(2, 0, two)
+        load_weight(2, 1, two)
+        load_weight(3, 0, one)
+        load_weight(3, 1, one)
         load_state(m_sb, m_prev, slice(2, TILES))
-        load_state(c_sb, c_prev, slice(0, TILES))
-        for pair in range(4, FIRST):
-            load_weight(pair, 0)
-            load_weight(pair, 1)
+        load_weight(3, 0, two)
+        load_weight(3, 1, two)
 
-        left, right = slice(0, SPLIT), slice(SPLIT, B)
         log_n(one)
-        group_act(0, on_scalar, left)
-        group_act(0, on_vector, right)
-        transpose_weights(0, 0)
-        empty_bank(0, 0, on_scalar)
-        quantise_act(0)
-        group_act(1, on_scalar, left)
-        group_act(1, on_vector, right)
-        transpose_weights(0, 1)
-        empty_bank(0, 1, on_scalar)
-        quantise_act(1)
-        group_act(2, on_scalar, left)
-        group_act(2, on_vector, right)
-        quantise_weights(0)
-        transpose_weights(1, 0)
-        empty_bank(1, 0, on_scalar)
-        quantise_act(2)
-        group_act(3, on_scalar, left)
-        group_act(3, on_vector, right)
-        transpose_weights(1, 1)
-        empty_bank(1, 1, on_scalar)
-        quantise_act(3)
-        transpose_weights(2, 0)
-        transpose_weights(2, 1)
-        empty_bank(2, 0, on_vector)
-        empty_bank(2, 1, on_vector)
-        nc.vector.tensor_copy(out=bias[:], in_=bias_raw[:, :, 0:TILES])
-        nc.vector.tensor_scalar(out=neg_bias_f[:], in0=bias[:, FORGET, :], scalar1=-1.0, scalar2=None, op0=ALU.mult)
+        for a in range(2 * PASSES):
+            side, e = divmod(a, 2)
+            if SPLIT:
+                group_act(a, on_scalar, left)
+            group_act(a, on_vector, right)
+            transpose_weights(0, side, e)
+            empty_bank(0, side, e, on_scalar)
+            quantise_act(a)
+            if e == 1:
+                quantise_weights(0, slice(side, side + 1))
+            if a == 2:
+                multiply(0, 0, 0)
+                multiply(0, 1, 0)
+        for tile in range(2, LT):
+            for side in range(2):
+                transpose_weights(tile // 2, side, tile % 2)
+                empty_bank(tile // 2, side, tile % 2, on_vector if HV else on_scalar)
+        multiply(0, 0, 1)
+        multiply(0, 1, 1)
 
-        single = lambda fn: (lambda j: fn(slice(j, j + 1)))
-        store_m = lambda js: nc.sync.dma_start(out=out_m[:, js, :], in_=lane_m[:, js, :])
-        store_n = lambda js: nc.sync.dma_start(out=out_n[:, js, :], in_=lane_n[:, js, :])
+        on_pair = lambda fn: (lambda k: fn(pair(k)))
 
-        for step in range(STEPS + 1):
-            ahead = step + LEAD
-            prep = ahead < STEPS
-            if step % 2 == 0 and FIRST + step // 2 < STEPS // 2:
-                load_weight(FIRST + step // 2, 0)
-                load_weight(FIRST + step // 2, 1)
-            if prep:
-                transpose_weights(ahead, 0)
-                transpose_weights(ahead, 1)
-            if step < STEPS:
-                multiply(step)
-            vector_banks = (1 if step in VB1 else 2) if step < 10 else 0
+        def both(fn):
+            return lambda k: (fn(2 * k), fn(2 * k + 1))
 
-            at(step, 17, tanh_wave)
-            at(step, S_N, new_n)
-            at(step, 25, sigmoid_wave)
-            if step + QL < STEPS:
-                quantise_weights(step + QL)
-            at(step, 1, min_f)
+        def at(first, fn):
+            k, odd = divmod(step - first, 2)
+            if not odd and 0 <= k < PAIRS:
+                fn(k)
+
+        def gap_and_m(k):
+            both(gap)(k)
+            clamp_gap(pair(k))
+            both(new_m)(k)
+
+        def quantise_round():
+            if step % 2 == Q_ODD and step // 2 + 1 < ROUNDS:
+                quantise_weights(step // 2 + 1)
+
+        for step in range(2 * ROUNDS + 1):
+            rnd = step // 2
+            if step % 2 == 0:
+                if rnd > 0 and FIRST + rnd - 1 < ROUNDS:
+                    load_weight(FIRST + rnd - 1, 0)
+                    load_weight(FIRST + rnd - 1, 1)
+                if rnd == 4:
+                    load_state(c_sb, c_prev, slice(0, TILES))
+            run = range(step, step + RUN) if step % RUN == 0 else ()
+            for s in run:
+                t = s + 3
+                if t < 2 * ROUNDS:
+                    transpose_weights(t // 2, 0, t % 2)
+                    transpose_weights(t // 2, 1, t % 2)
+            for s in run:
+                if 1 < s < 2 * ROUNDS:
+                    multiply(s // 2, s % 2, 0)
+                    multiply(s // 2, s % 2, 1)
+            vb = VB[step] if step < len(VB) else 0
+
+            def empty(side):
+                t = step + 3
+                if t < 2 * ROUNDS:
+                    empty_bank(t // 2, side, t % 2, on_vector if side >= 2 - vb else on_scalar)
+
+            if step == 1:
+                nc.vector.tensor_copy(out=bias[:], in_=bias_raw[:, :, 0:TILES])
+            at(2, both(min_f)) if step < 8 else None
+            at(18, both(tanh_wave))
+            if step < 2 * ROUNDS:
+                at(26, both(sigmoid_wave))
             if step == 0:
                 log_n(slice(1, 4))
             if step == 1:
                 log_n(slice(4, TILES))
-            if step == 3:
-                exp_f(slice(0, 2))
-            at(step, 2, single(exp_f)) if 3 < step < 9 else None
-            at(step, 1, abs_f)
-            if step == 10:
-                carry(0)
-            at(step, 9, carry) if step > 9 else None
-            at(step, S_NS, log_new_n)
-            at(step, S_U, log_gain)
-            at(step, 10, gap)
-            at(step, S_T, gained)
-            at(step, S_M, new_m)
-            at(step, S_R, ratio)
-            at(step, 25, new_h)
+            at(2, both(abs_f)) if step < 8 else None
             if step == 8:
+                abs_f(7)
+                min_f(6)
                 exp_f(slice(7, 8))
-            if step == 9:
-                log_f(slice(0, 2))
-            pair_at(step, 8, log_f, every=1) if step > 8 else None
-            at(step, S_E, gain)
-            if prep:
-                for side in range(2):
-                    empty_bank(ahead, side, on_vector if side < vector_banks else on_scalar)
-            pair_at(step, S_G, inv_n, every=1)
-            pair_at(step, S_CG, c_over_n, every=E_CG)
-            at(step, S_R, tanh_ratio)
-            at(step, S_C, new_c)
-            pair_at(step, S_M + 2, store_m)
-            pair_at(step, S_N + 2, store_n)
+                min_f(7)
+                log_f(pair(0))
+            if step >= Q_EARLY:
+                quantise_round()
+            if step == 0:
+                for j in range(TILES):
+                    one_plus_n(slice(j, j + 1))
+            at(S_D, gap_and_m)
+            at(S_R, ratio)
+            at(S_T, gained)
+            at(S_N, new_n)
+            at(S_F, on_pair(forget_prime))
+            empty(0)
+            empty(1)
+            if step == 1:
+                nc.vector.tensor_scalar(out=neg_bias_f[:], in0=bias[:, FORGET, :], scalar1=-1.0, scalar2=None, op0=ALU.mult)
+            for k in range(PAIRS):
+                if S_G[k] == step:
+                    inv_n(pair(k))
+            at(3, on_pair(exp_f)) if step < 8 else None
+            if step == 7:
+                abs_f(6)
+                exp_f(slice(6, 7))
+            if step in S_L:
+                log_f(pair(1 + S_L.index(step)))
+            at(S_E, on_pair(gain))
+            at(S_R, tanh_ratio)
+            at(S_W, cell)
+            if step < Q_EARLY:
+                quantise_round()
+            at(S_D - 1, both(carry))
+            at(S_C, new_c)
+            at(S_D + 1, store_m)
+            if step < 2 * ROUNDS:
+                at(S_H, on_pair(new_h))
+        for j in (TILES - 2, TILES - 1):
+            sigmoid_wave(j)
+            new_h(slice(j, j + 1))

@@ -21,30 +21,26 @@ PASSES = K // K_PASS
 TILES = H // P
 PAIRS = TILES // 2
 FORGET, INPUT, Z, OUTPUT = range(4)
-ROUNDS = 4 * PAIRS
+STEPS = 4 * TILES
+ROUNDS = STEPS // 2
+GAP_LIMIT = 80.0
+
 RAW_BUFS = 12
-EXP_CAP = 80.0
-ON_POOL = True
-LT = 3
-SPLIT = 192
-FIRST = 4
-VB = (0, 1, 2, 2, 2, 2, 2, 2, 2, 2)
-Q_ODD = 1
-S_D = 11
-S_L = (9, 10, 11)
-S_F = 13
-S_E = 17
-S_T = 19
-S_W = 20
-S_R = 24
-S_N = 16
-S_C = 24
-S_H = 26
-S_G = (3, 4, 5, 14)
-Q_EARLY = 99
-HV = 0
-RUN = 2
-VB = (0, 2, 2, 2, 2, 2, 2, 2, 2, 2)
+PRELOADED = RAW_BUFS // 2
+LEAD = 3
+SCALAR_COLS = 256
+
+READ = 2
+LOG_F = TILES
+CARRY = LOG_F + 2
+GAP = CARRY + 1
+EXP_GAP = 14
+NEW_N = EXP_GAP + 2
+INNER = Z * TILES + READ + 1
+RATIO = OUTPUT * TILES
+NEW_H = OUTPUT * TILES + READ
+INV_N_STEPS = (4, 5, 6, RATIO - 1)
+VECTOR_EMPTIES = range(READ, CARRY)
 
 
 def tile_slstmcell_pa_kernel(tc, x, h_prev, c_prev, n_prev, m_prev,
@@ -53,16 +49,25 @@ def tile_slstmcell_pa_kernel(tc, x, h_prev, c_prev, n_prev, m_prev,
                                          b_input, b_forget, b_output, b_z,
                                          out_h, out_c, out_n, out_m):
     nc = tc.nc
-    by_tile = lambda t: t.rearrange("(p j) c -> p j c", j=TILES)
+
+    def by_tile(t):
+        return t.rearrange("(p j) c -> p j c", j=TILES)
+
+    def pair(k):
+        return slice(2 * k, 2 * k + 2)
+
+    def tile(j):
+        return slice(j, j + 1)
+
     weights = [(by_tile(w), by_tile(r)) for w, r in
                ((w_forget, r_forget), (w_input, r_input), (w_z, r_z), (w_output, r_output))]
+    moving = (x, h_prev)
     biases = (b_forget, b_input, b_z, b_output)
-    acts = (x, h_prev)
     out_h, out_c, out_n, out_m = by_tile(out_h), by_tile(out_c), by_tile(out_n), by_tile(out_m)
 
     with ExitStack() as ctx:
         keep = ctx.enter_context(tc.tile_pool(name="keep", bufs=1))
-        stream = ctx.enter_context(tc.tile_pool(name="stream", bufs=2))
+        stream = ctx.enter_context(tc.tile_pool(name="stream", bufs=3))
         psum = ctx.enter_context(tc.psum_pool(name="psum", bufs=4))
         ctx.enter_context(tc.manual_schedule())
 
@@ -73,86 +78,103 @@ def tile_slstmcell_pa_kernel(tc, x, h_prev, c_prev, n_prev, m_prev,
         c_sb = keep.tile([P, TILES, B], BF16, name="c_sb")
         n_sb = keep.tile([P, TILES, B], BF16, name="n_sb")
         m_sb = keep.tile([P, TILES, B], BF16, name="m_sb")
-        act_codes = keep.tile([P, 2 * PASSES, B], U32, name="act_codes", align_bytes=64)
-        act_scales = keep.tile([P, 2 * PASSES, B], U8, name="act_scales", align_bytes=64)
-        lane_t = keep.tile([P, TILES, B], F32, name="lane_t")
-        lane_m = keep.tile([P, TILES, B], F32, name="lane_m")
-        lane_n = keep.tile([P, TILES, B], F32, name="lane_n")
-        lane_1 = keep.tile([P, TILES, B], F32, name="lane_1")
-        lane_r = keep.tile([P, TILES, B], F32, name="lane_r")
+        mov_codes = keep.tile([P, 2 * PASSES, B], U32, name="mov_codes", align_bytes=64)
+        mov_scales = keep.tile([P, 2 * PASSES, B], U8, name="mov_scales", align_bytes=64)
 
-        w_raw, banks, w_grouped, w_mx, waves, act_raw, act_grouped, tanh_z, sig_o = {}, {}, {}, {}, {}, {}, {}, {}, {}
-        pair = lambda k: slice(2 * k, 2 * k + 2)
+        abs_f = exp_f = ln_f = gap = exp_gap = gained = inner = keep.tile([P, TILES, B], F32, name="work_gap")
+        min_f = carry = m_new = keep.tile([P, TILES, B], F32, name="work_m")
+        exp_neg_gap = c_new = keep.tile([P, TILES, B], F32, name="work_c")
+        n_plus_1 = n_new = keep.tile([P, TILES, B], F32, name="work_n")
+        ln_n = inv_n = ratio = tanh_ratio = h_new = keep.tile([P, TILES, B], F32, name="work_h")
 
-        def load_weight(rnd, side, s=slice(0, 2)):
-            gate, j0 = divmod(2 * rnd, TILES)
+        w_raw, turned, w_grouped, w_mx, waves = {}, {}, {}, {}, {}
+        mov_raw, mov_grouped, tanh_z, sigmoid_o = {}, {}, {}, {}
+
+        def load_weights(rnd, side, which=slice(0, 2)):
+            gate, first = divmod(2 * rnd, TILES)
             if (rnd, side) not in w_raw:
                 w_raw[rnd, side] = stream.tile([P, 2, K], BF16, name="raw", bufs=RAW_BUFS)
-            nc.sync.dma_start(out=w_raw[rnd, side][:, s, :], in_=weights[gate][side][:, j0 + s.start:j0 + s.stop, :])
+            nc.sync.dma_start(out=w_raw[rnd, side][:, which, :],
+                              in_=weights[gate][side][:, first + which.start:first + which.stop, :])
 
-        def load_act(a):
+        def load_weight_tile(step):
+            for side in range(2):
+                load_weights(step // 2, side, tile(step % 2))
+
+        def load_moving(a):
             side, g = divmod(a, PASSES)
-            act_raw[a] = stream.tile([P, PACK, B], BF16, name="raw", bufs=RAW_BUFS)
-            nc.sync.dma_start(out=act_raw[a][:], in_=acts[side][g * K_PASS:(g + 1) * K_PASS, :].rearrange("(p t) b -> p t b", t=PACK))
+            mov_raw[a] = stream.tile([P, PACK, B], BF16, name="raw", bufs=RAW_BUFS)
+            rows = moving[side][g * K_PASS:(g + 1) * K_PASS, :]
+            nc.sync.dma_start(out=mov_raw[a][:], in_=rows.rearrange("(p t) b -> p t b", t=PACK))
 
         def load_state(dst, src, js):
             nc.sync.dma_start(out=dst[:, js, :], in_=by_tile(src)[:, js, :])
 
         def load_biases():
             for gate in range(4):
-                nc.sync.dma_start(out=bias_raw[:, gate, 0:TILES], in_=biases[gate].rearrange("(p j) -> p j", j=TILES))
+                nc.sync.dma_start(out=bias_raw[:, gate, 0:TILES],
+                                  in_=biases[gate].rearrange("(p j) -> p j", j=TILES))
 
-        def group_act(a, copy, cols):
-            if a not in act_grouped:
-                act_grouped[a] = stream.tile([P, B, PACK], BF16, name="act_grouped", bufs=3, align_bytes=64)
-            copy(out=act_grouped[a][:, cols, :].rearrange("p (c i) t -> p c t i", i=4),
-                 in_=act_raw[a][:, :, cols].rearrange("p t (c i) -> p c t i", i=4))
+        def store(dst, src, js):
+            nc.sync.dma_start(out=dst[:, js, :], in_=src[:, js, :])
 
-        def quantise_act(a):
-            nc.vector.quantize_mx(out=act_codes[:, a, :].bitcast(E5M2X4), scales=act_scales[:, a, :],
-                                  in_=act_grouped[a][:].rearrange("p b t -> p (b t)"))
+        def group_moving(a, copy, cols):
+            if a not in mov_grouped:
+                mov_grouped[a] = stream.tile([P, B, PACK], BF16, name="mov_grouped", align_bytes=64)
+            copy(out=mov_grouped[a][:, cols, :].rearrange("p (c i) t -> p c t i", i=4),
+                 in_=mov_raw[a][:, :, cols].rearrange("p t (c i) -> p c t i", i=4))
 
-        def transpose_weights(rnd, side, e):
-            words = w_raw[rnd, side][:, e, :].bitcast(F32)
-            bank = psum.tile([P, PASSES, 2, P], F32, name="turned")
-            banks[rnd, side, e] = bank
+        def quantise_moving(a):
+            nc.vector.quantize_mx(out=mov_codes[:, a, :].bitcast(E5M2X4), scales=mov_scales[:, a, :],
+                                  in_=mov_grouped[a][:].rearrange("p b t -> p (b t)"))
+
+        def transpose_weights(step, side):
+            words = w_raw[step // 2, side][:, step % 2, :].bitcast(F32)
+            turned[step, side] = psum.tile([P, PASSES, 2, P], F32, name="turned")
             for g in range(PASSES):
                 for u in range(2):
-                    nc.tensor.transpose(bank[:, g, u, :], words[:, 2 * P * g + u:2 * P * (g + 1):2], ident[:])
+                    nc.tensor.transpose(turned[step, side][:, g, u, :],
+                                        words[:, 2 * P * g + u:2 * P * (g + 1):2], ident[:])
 
-        def empty_bank(rnd, side, e, copy):
+        def empty_bank(step, side, copy):
+            rnd = step // 2
             if rnd not in w_grouped:
-                w_grouped[rnd] = stream.tile([P, 2, 2, PASSES * P * PACK], BF16, name="w_grouped", bufs=3, align_bytes=64)
-            dst = w_grouped[rnd][:, side, e, :].bitcast(F32).rearrange("p (g r u) -> p g r u", g=PASSES, u=2)
-            copy(out=dst, in_=banks[rnd, side, e][:].rearrange("p g u r -> p g r u"))
+                w_grouped[rnd] = stream.tile([P, 2, 2, PASSES * P * PACK], BF16, name="w_grouped", align_bytes=64)
+            dst = w_grouped[rnd][:, side, step % 2, :].bitcast(F32)
+            copy(out=dst.rearrange("p (g r u) -> p g r u", g=PASSES, u=2),
+                 in_=turned[step, side][:].rearrange("p g u r -> p g r u"))
 
         def quantise_weights(rnd, sides=slice(0, 2)):
             if rnd not in w_mx:
-                codes = stream.tile([P, 2, 2 * PASSES * P], U32, name="w_codes", bufs=3, align_bytes=64)
-                scales = stream.tile([P, 2, 2 * PASSES * P], U8, name="w_scales", bufs=3, align_bytes=64)
-                w_mx[rnd] = codes, scales
-            codes, scales = w_mx[rnd]
-            nc.vector.quantize_mx(out=codes[:, sides, :].rearrange("p s c -> p (s c)").bitcast(E5M2X4),
-                                  scales=scales[:, sides, :].rearrange("p s c -> p (s c)"),
+                w_codes = stream.tile([P, 2, 2 * PASSES * P], U32, name="w_codes", align_bytes=64)
+                w_scales = stream.tile([P, 2, 2 * PASSES * P], U8, name="w_scales", align_bytes=64)
+                w_mx[rnd] = w_codes, w_scales
+            w_codes, w_scales = w_mx[rnd]
+            nc.vector.quantize_mx(out=w_codes[:, sides, :].rearrange("p s c -> p (s c)").bitcast(E5M2X4),
+                                  scales=w_scales[:, sides, :].rearrange("p s c -> p (s c)"),
                                   in_=w_grouped[rnd][:, sides, :, :].rearrange("p s e c -> p (s e c)"))
 
-        def multiply(rnd, e, side):
-            codes, scales = w_mx[rnd]
+        def multiply(step, side):
+            w_codes, w_scales = w_mx[step // 2]
             if side == 0:
-                waves[2 * rnd + e] = psum.tile([P, B], F32, name="wave")
+                waves[step] = psum.tile([P, B], F32, name="wave")
             for g in range(PASSES):
-                cols = slice((e * PASSES + g) * P, (e * PASSES + g + 1) * P)
-                a = side * PASSES + g
-                nc.tensor.matmul_mx(out=waves[2 * rnd + e][:],
-                                    lhsT=codes[:, side, cols].bitcast(E5M2X4), lhsT_scale=scales[:, side, cols],
-                                    rhs=act_codes[:, a, :].bitcast(E5M2X4), rhs_scale=act_scales[:, a, :],
+                first = ((step % 2) * PASSES + g) * P
+                a = PASSES * side + g
+                nc.tensor.matmul_mx(out=waves[step][:],
+                                    lhsT=w_codes[:, side, first:first + P].bitcast(E5M2X4),
+                                    lhsT_scale=w_scales[:, side, first:first + P],
+                                    rhs=mov_codes[:, a, :].bitcast(E5M2X4), rhs_scale=mov_scales[:, a, :],
                                     start=(a == 0), stop=(a == 2 * PASSES - 1))
 
-        def col(gate, j):
+        def wave(gate, j):
+            return waves[gate * TILES + j]
+
+        def bias_of(gate, j):
             return bias[:, gate, j:j + 1]
 
-        def act(out, in_, func, **kw):
-            nc.scalar.activation(out=out, in_=in_, func=func, **kw)
+        def act(out, in_, func, **affine):
+            nc.scalar.activation(out=out, in_=in_, func=func, **affine)
 
         def stt(out, in0, scalar, op0, op1, in1):
             nc.vector.scalar_tensor_tensor(out=out, in0=in0, scalar=scalar, in1=in1, op0=op0, op1=op1)
@@ -160,232 +182,194 @@ def tile_slstmcell_pa_kernel(tc, x, h_prev, c_prev, n_prev, m_prev,
         def tt(out, in0, op, in1):
             nc.vector.tensor_tensor(out=out, in0=in0, in1=in1, op=op)
 
-        clamp_engine = nc.gpsimd if ON_POOL else nc.vector
+        def do_n_plus_1(js):
+            nc.gpsimd.tensor_scalar(out=n_plus_1[:, js, :], in0=n_sb[:, js, :], scalar1=1.0, scalar2=1.0,
+                                    op0=ALU.add, op1=ALU.mult)
 
-        def abs_f(j):
-            act(lane_t[:, j, :], waves[j][:], ACT.Abs, bias=col(FORGET, j))
+        def do_ln_n(js):
+            act(ln_n[:, js, :], n_sb[:, js, :], ACT.Ln, bias=1.0)
 
-        def min_f(j):
-            stt(lane_m[:, j, :], waves[j][:], neg_bias_f[:, j:j + 1], ALU.min, ALU.add, m_sb[:, j, :])
+        def do_inv_n(k):
+            act(inv_n[:, pair(k), :], ln_n[:, pair(k), :], ACT.Exp, scale=-1.0)
 
-        def log_n(js):
-            act(lane_r[:, js, :], n_sb[:, js, :], ACT.Ln, bias=1.0)
+        def do_abs_f(j):
+            act(abs_f[:, j, :], wave(FORGET, j)[:], ACT.Abs, bias=bias_of(FORGET, j))
 
-        def exp_f(js):
-            act(lane_t[:, js, :], lane_t[:, js, :], ACT.Exp, scale=-1.0)
+        def do_min_f(j):
+            stt(min_f[:, j, :], wave(FORGET, j)[:], neg_bias_f[:, j:j + 1], ALU.min, ALU.add, m_sb[:, j, :])
 
-        def log_f(js):
-            act(lane_t[:, js, :], lane_t[:, js, :], ACT.Ln, bias=1.0)
+        def do_exp_f(js):
+            act(exp_f[:, js, :], abs_f[:, js, :], ACT.Exp, scale=-1.0)
 
-        def inv_n(js):
-            act(lane_r[:, js, :], lane_r[:, js, :], ACT.Exp, scale=-1.0)
+        def do_ln_f(k):
+            act(ln_f[:, pair(k), :], exp_f[:, pair(k), :], ACT.Ln, bias=1.0)
 
-        def carry(j):
-            stt(lane_m[:, j, :], lane_m[:, j, :], col(FORGET, j), ALU.add, ALU.subtract, lane_t[:, j, :])
+        def do_carry(j):
+            stt(carry[:, j, :], min_f[:, j, :], bias_of(FORGET, j), ALU.add, ALU.subtract, ln_f[:, j, :])
 
-        def gap(j):
-            stt(lane_t[:, j, :], waves[TILES + j][:], col(INPUT, j), ALU.add, ALU.subtract, lane_m[:, j, :])
+        def do_gap_and_m(k):
+            for j in (2 * k, 2 * k + 1):
+                stt(gap[:, j, :], wave(INPUT, j)[:], bias_of(INPUT, j), ALU.add, ALU.subtract, carry[:, j, :])
+                nc.gpsimd.tensor_scalar(out=gap[:, j, :], in0=gap[:, j, :], scalar1=GAP_LIMIT,
+                                        scalar2=-GAP_LIMIT, op0=ALU.min, op1=ALU.max)
+            for j in (2 * k, 2 * k + 1):
+                stt(m_new[:, j, :], wave(INPUT, j)[:], bias_of(INPUT, j), ALU.add, ALU.max, carry[:, j, :])
 
-        def new_m(j):
-            stt(lane_m[:, j, :], waves[TILES + j][:], col(INPUT, j), ALU.add, ALU.max, lane_m[:, j, :])
+        def do_exp_neg_gap(k):
+            act(exp_neg_gap[:, pair(k), :], gap[:, pair(k), :], ACT.Exp, scale=-1.0)
 
-        def clamp_gap(js):
-            clamp_engine.tensor_scalar(out=lane_t[:, js, :], in0=lane_t[:, js, :], scalar1=EXP_CAP, scalar2=-EXP_CAP, op0=ALU.min, op1=ALU.max)
+        def do_exp_gap(k):
+            act(exp_gap[:, pair(k), :], gap[:, pair(k), :], ACT.Exp)
 
-        def one_plus_n(js):
-            clamp_engine.tensor_scalar(out=lane_1[:, js, :], in0=n_sb[:, js, :], scalar1=1.0, scalar2=1.0, op0=ALU.add, op1=ALU.mult)
+        def do_n_new(k):
+            stt(n_new[:, pair(k), :], exp_neg_gap[:, pair(k), :], 1.0, ALU.min, ALU.mult, n_plus_1[:, pair(k), :])
+            store(out_n, n_new, pair(k))
 
-        def gain(js):
-            act(lane_t[:, js, :], lane_t[:, js, :], ACT.Exp)
+        def do_tanh_z(k):
+            tanh_z[k] = stream.tile([P, 2, B], F32, name="gate_value")
+            for e in range(2):
+                act(tanh_z[k][:, e, :], wave(Z, 2 * k + e)[:], ACT.Tanh, bias=bias_of(Z, 2 * k + e))
 
-        def forget_prime(js):
-            act(lane_n[:, js, :], lane_t[:, js, :], ACT.Exp, scale=-1.0)
+        def do_gained(k):
+            tt(gained[:, pair(k), :], exp_gap[:, pair(k), :], ALU.mult, tanh_z[k][:])
 
-        def tanh_wave(j):
-            if j % 2 == 0:
-                tanh_z[j // 2] = stream.tile([P, 2, B], F32, name="wave_sb", bufs=3)
-            act(tanh_z[j // 2][:, j % 2, :], waves[2 * TILES + j][:], ACT.Tanh, bias=col(Z, j))
+        def do_inner(k):
+            tt(inner[:, pair(k), :], gained[:, pair(k), :], ALU.add, c_sb[:, pair(k), :])
 
-        def gained(k):
-            tt(lane_t[:, pair(k), :], lane_t[:, pair(k), :], ALU.mult, tanh_z[k][:])
+        def do_ratio(k):
+            tt(ratio[:, pair(k), :], inv_n[:, pair(k), :], ALU.mult, inner[:, pair(k), :])
 
-        def cell(k):
-            tt(lane_t[:, pair(k), :], lane_t[:, pair(k), :], ALU.add, c_sb[:, pair(k), :])
+        def do_tanh_ratio(k):
+            act(tanh_ratio[:, pair(k), :], ratio[:, pair(k), :], ACT.Tanh)
 
-        def ratio(k):
-            tt(lane_r[:, pair(k), :], lane_r[:, pair(k), :], ALU.mult, lane_t[:, pair(k), :])
+        def do_c_new(k):
+            stt(c_new[:, pair(k), :], exp_neg_gap[:, pair(k), :], 1.0, ALU.min, ALU.mult, inner[:, pair(k), :])
+            store(out_c, c_new, pair(k))
 
-        def new_c(k):
-            stt(lane_t[:, pair(k), :], lane_n[:, pair(k), :], 1.0, ALU.min, ALU.mult, lane_t[:, pair(k), :])
-            nc.sync.dma_start(out=out_c[:, pair(k), :], in_=lane_t[:, pair(k), :])
+        def do_sigmoid_o(j, cols=slice(0, B)):
+            if j // 2 not in sigmoid_o:
+                sigmoid_o[j // 2] = stream.tile([P, 2, B], F32, name="gate_value")
+            act(sigmoid_o[j // 2][:, j % 2, cols], wave(OUTPUT, j)[:, cols], ACT.Sigmoid, bias=bias_of(OUTPUT, j))
 
-        def new_n(k):
-            stt(lane_1[:, pair(k), :], lane_n[:, pair(k), :], 1.0, ALU.min, ALU.mult, lane_1[:, pair(k), :])
-            nc.sync.dma_start(out=out_n[:, pair(k), :], in_=lane_1[:, pair(k), :])
-
-        def store_m(k):
-            nc.sync.dma_start(out=out_m[:, pair(k), :], in_=lane_m[:, pair(k), :])
-
-        def tanh_ratio(k):
-            act(lane_r[:, pair(k), :], lane_r[:, pair(k), :], ACT.Tanh)
-
-        def sigmoid_wave(j):
-            if j % 2 == 0:
-                sig_o[j // 2] = stream.tile([P, 2, B], F32, name="wave_sb", bufs=3)
-            act(sig_o[j // 2][:, j % 2, :], waves[3 * TILES + j][:], ACT.Sigmoid, bias=col(OUTPUT, j))
-
-        def new_h(js):
-            k = js.start // 2
-            tt(lane_r[:, js, :], lane_r[:, js, :], ALU.mult, sig_o[k][:, js.start - 2 * k:js.stop - 2 * k, :])
-            nc.sync.dma_start(out=out_h[:, js, :], in_=lane_r[:, js, :])
-
-        on_scalar, on_vector = nc.scalar.copy, nc.vector.tensor_copy
-        one, two = slice(0, 1), slice(1, 2)
-        left, right = slice(0, SPLIT), slice(SPLIT, B)
-
-        make_identity(nc, ident[:])
-        load_state(n_sb, n_prev, one)
-        load_act(0)
-        load_weight(0, 0, one)
-        load_act(1)
-        load_weight(0, 0, two)
-        load_act(2)
-        load_weight(0, 1, one)
-        load_act(3)
-        load_weight(0, 1, two)
-        load_weight(1, 0, one)
-        load_weight(1, 1, one)
-        load_weight(1, 0, two)
-        load_weight(1, 1, two)
-        load_state(n_sb, n_prev, slice(1, 4))
-        load_state(n_sb, n_prev, slice(4, TILES))
-        load_biases()
-        load_weight(2, 0, one)
-        load_weight(2, 1, one)
-        load_state(m_sb, m_prev, pair(0))
-        load_weight(2, 0, two)
-        load_weight(2, 1, two)
-        load_weight(3, 0, one)
-        load_weight(3, 1, one)
-        load_state(m_sb, m_prev, slice(2, TILES))
-        load_weight(3, 0, two)
-        load_weight(3, 1, two)
-
-        log_n(one)
-        for a in range(2 * PASSES):
-            side, e = divmod(a, 2)
-            if SPLIT:
-                group_act(a, on_scalar, left)
-            group_act(a, on_vector, right)
-            transpose_weights(0, side, e)
-            empty_bank(0, side, e, on_scalar)
-            quantise_act(a)
-            if e == 1:
-                quantise_weights(0, slice(side, side + 1))
-            if a == 2:
-                multiply(0, 0, 0)
-                multiply(0, 1, 0)
-        for tile in range(2, LT):
-            for side in range(2):
-                transpose_weights(tile // 2, side, tile % 2)
-                empty_bank(tile // 2, side, tile % 2, on_vector if HV else on_scalar)
-        multiply(0, 0, 1)
-        multiply(0, 1, 1)
-
-        on_pair = lambda fn: (lambda k: fn(pair(k)))
+        def do_h_new(k):
+            tt(h_new[:, pair(k), :], tanh_ratio[:, pair(k), :], ALU.mult, sigmoid_o[k][:])
+            store(out_h, h_new, pair(k))
 
         def both(fn):
             return lambda k: (fn(2 * k), fn(2 * k + 1))
 
-        def at(first, fn):
+        on_scalar, on_vector = nc.scalar.copy, nc.vector.tensor_copy
+
+        make_identity(nc, ident[:])
+        load_state(n_sb, n_prev, tile(0))
+        for a in range(2 * PASSES):
+            load_moving(a)
+            load_weights(0, a // 2, tile(a % 2))
+        load_weight_tile(2)
+        load_weight_tile(3)
+        load_state(n_sb, n_prev, slice(1, TILES // 2))
+        load_biases()
+        load_weight_tile(4)
+        load_state(n_sb, n_prev, slice(TILES // 2, TILES))
+        load_state(m_sb, m_prev, pair(0))
+        load_weight_tile(5)
+        load_weight_tile(6)
+        load_state(m_sb, m_prev, slice(2, TILES))
+        load_weight_tile(7)
+        for rnd in range(PAIRS, PRELOADED):
+            load_weights(rnd, 0)
+            load_weights(rnd, 1)
+
+        do_ln_n(tile(0))
+        for a in range(2 * PASSES):
+            side, e = divmod(a, 2)
+            group_moving(a, on_scalar, slice(0, SCALAR_COLS))
+            group_moving(a, on_vector, slice(SCALAR_COLS, B))
+            transpose_weights(e, side)
+            empty_bank(e, side, on_scalar)
+            quantise_moving(a)
+            if e == 1:
+                quantise_weights(0, slice(side, side + 1))
+            if a == PASSES:
+                multiply(0, 0)
+                multiply(1, 0)
+        for side in range(2):
+            transpose_weights(LEAD - 1, side)
+            empty_bank(LEAD - 1, side, on_vector)
+        multiply(0, 1)
+        multiply(1, 1)
+
+        def at(first, fn, count=PAIRS):
             k, odd = divmod(step - first, 2)
-            if not odd and 0 <= k < PAIRS:
+            if not odd and 0 <= k < count:
                 fn(k)
 
-        def gap_and_m(k):
-            both(gap)(k)
-            clamp_gap(pair(k))
-            both(new_m)(k)
-
-        def quantise_round():
-            if step % 2 == Q_ODD and step // 2 + 1 < ROUNDS:
-                quantise_weights(step // 2 + 1)
-
-        for step in range(2 * ROUNDS + 1):
-            rnd = step // 2
-            if step % 2 == 0:
-                if rnd > 0 and FIRST + rnd - 1 < ROUNDS:
-                    load_weight(FIRST + rnd - 1, 0)
-                    load_weight(FIRST + rnd - 1, 1)
-                if rnd == 4:
+        last_f = TILES - 1
+        for step in range(STEPS + 1):
+            rnd, second = divmod(step, 2)
+            if not second:
+                if 0 < rnd <= ROUNDS - PRELOADED:
+                    load_weights(PRELOADED + rnd - 1, 0)
+                    load_weights(PRELOADED + rnd - 1, 1)
+                if rnd == PAIRS - 1:
                     load_state(c_sb, c_prev, slice(0, TILES))
-            run = range(step, step + RUN) if step % RUN == 0 else ()
-            for s in run:
-                t = s + 3
-                if t < 2 * ROUNDS:
-                    transpose_weights(t // 2, 0, t % 2)
-                    transpose_weights(t // 2, 1, t % 2)
-            for s in run:
-                if 1 < s < 2 * ROUNDS:
-                    multiply(s // 2, s % 2, 0)
-                    multiply(s // 2, s % 2, 1)
-            vb = VB[step] if step < len(VB) else 0
-
-            def empty(side):
-                t = step + 3
-                if t < 2 * ROUNDS:
-                    empty_bank(t // 2, side, t % 2, on_vector if side >= 2 - vb else on_scalar)
+                for ahead in range(step + LEAD, min(step + LEAD + 2, STEPS)):
+                    transpose_weights(ahead, 0)
+                    transpose_weights(ahead, 1)
+                if 0 < rnd < ROUNDS:
+                    for s in (step, step + 1):
+                        multiply(s, 0)
+                        multiply(s, 1)
 
             if step == 1:
                 nc.vector.tensor_copy(out=bias[:], in_=bias_raw[:, :, 0:TILES])
-            at(2, both(min_f)) if step < 8 else None
-            at(18, both(tanh_wave))
-            if step < 2 * ROUNDS:
-                at(26, both(sigmoid_wave))
+            at(READ, both(do_min_f), PAIRS - 1)
+            at(Z * TILES + READ, do_tanh_z)
+            at(NEW_H, both(do_sigmoid_o), PAIRS - 1)
             if step == 0:
-                log_n(slice(1, 4))
+                do_ln_n(slice(1, TILES // 2))
             if step == 1:
-                log_n(slice(4, TILES))
-            at(2, both(abs_f)) if step < 8 else None
-            if step == 8:
-                abs_f(7)
-                min_f(6)
-                exp_f(slice(7, 8))
-                min_f(7)
-                log_f(pair(0))
-            if step >= Q_EARLY:
-                quantise_round()
+                do_ln_n(slice(TILES // 2, TILES))
+            at(READ, both(do_abs_f), PAIRS - 1)
+            if step == LOG_F:
+                do_abs_f(last_f)
+                do_min_f(last_f - 1)
+                do_exp_f(tile(last_f))
+                do_min_f(last_f)
+                do_ln_f(0)
             if step == 0:
                 for j in range(TILES):
-                    one_plus_n(slice(j, j + 1))
-            at(S_D, gap_and_m)
-            at(S_R, ratio)
-            at(S_T, gained)
-            at(S_N, new_n)
-            at(S_F, on_pair(forget_prime))
-            empty(0)
-            empty(1)
+                    do_n_plus_1(tile(j))
+            at(GAP, do_gap_and_m)
+            at(RATIO, do_ratio)
+            at(INNER, do_gained)
+            at(NEW_N, do_n_new)
+            at(EXP_GAP, do_exp_neg_gap)
+            if step + LEAD < STEPS:
+                for side in range(2):
+                    empty_bank(step + LEAD, side, on_vector if step in VECTOR_EMPTIES else on_scalar)
             if step == 1:
-                nc.vector.tensor_scalar(out=neg_bias_f[:], in0=bias[:, FORGET, :], scalar1=-1.0, scalar2=None, op0=ALU.mult)
-            for k in range(PAIRS):
-                if S_G[k] == step:
-                    inv_n(pair(k))
-            at(3, on_pair(exp_f)) if step < 8 else None
-            if step == 7:
-                abs_f(6)
-                exp_f(slice(6, 7))
-            if step in S_L:
-                log_f(pair(1 + S_L.index(step)))
-            at(S_E, on_pair(gain))
-            at(S_R, tanh_ratio)
-            at(S_W, cell)
-            if step < Q_EARLY:
-                quantise_round()
-            at(S_D - 1, both(carry))
-            at(S_C, new_c)
-            at(S_D + 1, store_m)
-            if step < 2 * ROUNDS:
-                at(S_H, on_pair(new_h))
-        for j in (TILES - 2, TILES - 1):
-            sigmoid_wave(j)
-            new_h(slice(j, j + 1))
+                nc.vector.tensor_scalar(out=neg_bias_f[:], in0=bias[:, FORGET, :], scalar1=-1.0, scalar2=None,
+                                        op0=ALU.mult)
+            if step in INV_N_STEPS:
+                do_inv_n(INV_N_STEPS.index(step))
+            at(READ + 1, lambda k: do_exp_f(pair(k)), PAIRS - 1)
+            if step == LOG_F - 1:
+                do_abs_f(last_f - 1)
+                do_exp_f(tile(last_f - 1))
+            if LOG_F < step < LOG_F + PAIRS:
+                do_ln_f(step - LOG_F)
+            at(EXP_GAP + 1, do_exp_gap)
+            at(RATIO, do_tanh_ratio)
+            at(INNER + 1, do_inner)
+            if second and rnd + 1 < ROUNDS:
+                quantise_weights(rnd + 1)
+            at(CARRY, both(do_carry))
+            at(RATIO, do_c_new)
+            at(GAP + 1, lambda k: store(out_m, m_new, pair(k)))
+            at(NEW_H, do_h_new, PAIRS - 1)
+
+        for j, cols in ((TILES - 2, slice(0, B)), (TILES - 1, slice(0, B // 2)), (TILES - 1, slice(B // 2, B))):
+            do_sigmoid_o(j, cols)
+            tt(h_new[:, j, cols], tanh_ratio[:, j, cols], ALU.mult, sigmoid_o[j // 2][:, j % 2, cols])
+            nc.sync.dma_start(out=out_h[:, j, cols], in_=h_new[:, j, cols])

from contextlib import ExitStack

import concourse.mybir as mybir
from concourse.masks import make_identity

H, K, B = 1024, 1024, 512
FLOPS = 8 * 2 * H * K * B

F32 = mybir.dt.float32
BF16 = mybir.dt.bfloat16
U32 = mybir.dt.uint32
U8 = mybir.dt.uint8
E5M2X4 = mybir.dt.float8_e5m2_x4
ALU = mybir.AluOpType
ACT = mybir.ActivationFunctionType

P = 128
PACK = 4
K_PASS = P * PACK
PASSES = K // K_PASS
TILES = H // P
PAIRS = TILES // 2
FORGET, INPUT, Z, OUTPUT = range(4)
STEPS = 4 * TILES
ROUNDS = STEPS // 2
GAP_LIMIT = 80.0

RAW_BUFS = 12
PRELOADED = RAW_BUFS // 2
LEAD = 3
SCALAR_COLS = 256

READ = 2
LOG_F = TILES
CARRY = LOG_F + 2
GAP = CARRY + 1
EXP_GAP = 14
NEW_N = EXP_GAP + 2
INNER = Z * TILES + READ + 1
RATIO = OUTPUT * TILES
NEW_H = OUTPUT * TILES + READ
INV_N_STEPS = (4, 5, 6, RATIO - 1)
VECTOR_EMPTIES = range(READ, CARRY)


def tile_slstmcell_pa_kernel(tc, x, h_prev, c_prev, n_prev, m_prev,
                                         w_input, w_forget, w_output, w_z,
                                         r_input, r_forget, r_output, r_z,
                                         b_input, b_forget, b_output, b_z,
                                         out_h, out_c, out_n, out_m):
    nc = tc.nc

    def by_tile(t):
        return t.rearrange("(p j) c -> p j c", j=TILES)

    def pair(k):
        return slice(2 * k, 2 * k + 2)

    def tile(j):
        return slice(j, j + 1)

    weights = [(by_tile(w), by_tile(r)) for w, r in
               ((w_forget, r_forget), (w_input, r_input), (w_z, r_z), (w_output, r_output))]
    moving = (x, h_prev)
    biases = (b_forget, b_input, b_z, b_output)
    out_h, out_c, out_n, out_m = by_tile(out_h), by_tile(out_c), by_tile(out_n), by_tile(out_m)

    with ExitStack() as ctx:
        keep = ctx.enter_context(tc.tile_pool(name="keep", bufs=1))
        stream = ctx.enter_context(tc.tile_pool(name="stream", bufs=3))
        psum = ctx.enter_context(tc.psum_pool(name="psum", bufs=4))
        ctx.enter_context(tc.manual_schedule())

        ident = keep.tile([P, P], F32, name="ident")
        bias_raw = keep.tile([P, 4, 2 * TILES], BF16, name="bias_raw")
        bias = keep.tile([P, 4, TILES], F32, name="bias")
        neg_bias_f = keep.tile([P, TILES], F32, name="neg_bias_f")
        c_sb = keep.tile([P, TILES, B], BF16, name="c_sb")
        n_sb = keep.tile([P, TILES, B], BF16, name="n_sb")
        m_sb = keep.tile([P, TILES, B], BF16, name="m_sb")
        mov_codes = keep.tile([P, 2 * PASSES, B], U32, name="mov_codes", align_bytes=64)
        mov_scales = keep.tile([P, 2 * PASSES, B], U8, name="mov_scales", align_bytes=64)

        abs_f = exp_f = ln_f = gap = exp_gap = gained = inner = keep.tile([P, TILES, B], F32, name="work_gap")
        min_f = carry = m_new = keep.tile([P, TILES, B], F32, name="work_m")
        exp_neg_gap = c_new = keep.tile([P, TILES, B], F32, name="work_c")
        n_plus_1 = n_new = keep.tile([P, TILES, B], F32, name="work_n")
        ln_n = inv_n = ratio = tanh_ratio = h_new = keep.tile([P, TILES, B], F32, name="work_h")

        w_raw, turned, w_grouped, w_mx, waves = {}, {}, {}, {}, {}
        mov_raw, mov_grouped, tanh_z, sigmoid_o = {}, {}, {}, {}

        def load_weights(rnd, side, which=slice(0, 2)):
            gate, first = divmod(2 * rnd, TILES)
            if (rnd, side) not in w_raw:
                w_raw[rnd, side] = stream.tile([P, 2, K], BF16, name="raw", bufs=RAW_BUFS)
            nc.sync.dma_start(out=w_raw[rnd, side][:, which, :],
                              in_=weights[gate][side][:, first + which.start:first + which.stop, :])

        def load_weight_tile(step):
            for side in range(2):
                load_weights(step // 2, side, tile(step % 2))

        def load_moving(a):
            side, g = divmod(a, PASSES)
            mov_raw[a] = stream.tile([P, PACK, B], BF16, name="raw", bufs=RAW_BUFS)
            rows = moving[side][g * K_PASS:(g + 1) * K_PASS, :]
            nc.sync.dma_start(out=mov_raw[a][:], in_=rows.rearrange("(p t) b -> p t b", t=PACK))

        def load_state(dst, src, js):
            nc.sync.dma_start(out=dst[:, js, :], in_=by_tile(src)[:, js, :])

        def load_biases():
            for gate in range(4):
                nc.sync.dma_start(out=bias_raw[:, gate, 0:TILES],
                                  in_=biases[gate].rearrange("(p j) -> p j", j=TILES))

        def store(dst, src, js):
            nc.sync.dma_start(out=dst[:, js, :], in_=src[:, js, :])

        def group_moving(a, copy, cols):
            if a not in mov_grouped:
                mov_grouped[a] = stream.tile([P, B, PACK], BF16, name="mov_grouped", align_bytes=64)
            copy(out=mov_grouped[a][:, cols, :].rearrange("p (c i) t -> p c t i", i=4),
                 in_=mov_raw[a][:, :, cols].rearrange("p t (c i) -> p c t i", i=4))

        def quantise_moving(a):
            nc.vector.quantize_mx(out=mov_codes[:, a, :].bitcast(E5M2X4), scales=mov_scales[:, a, :],
                                  in_=mov_grouped[a][:].rearrange("p b t -> p (b t)"))

        def transpose_weights(step, side):
            words = w_raw[step // 2, side][:, step % 2, :].bitcast(F32)
            turned[step, side] = psum.tile([P, PASSES, 2, P], F32, name="turned")
            for g in range(PASSES):
                for u in range(2):
                    nc.tensor.transpose(turned[step, side][:, g, u, :],
                                        words[:, 2 * P * g + u:2 * P * (g + 1):2], ident[:])

        def empty_bank(step, side, copy):
            rnd = step // 2
            if rnd not in w_grouped:
                w_grouped[rnd] = stream.tile([P, 2, 2, PASSES * P * PACK], BF16, name="w_grouped", align_bytes=64)
            dst = w_grouped[rnd][:, side, step % 2, :].bitcast(F32)
            copy(out=dst.rearrange("p (g r u) -> p g r u", g=PASSES, u=2),
                 in_=turned[step, side][:].rearrange("p g u r -> p g r u"))

        def quantise_weights(rnd, sides=slice(0, 2)):
            if rnd not in w_mx:
                w_codes = stream.tile([P, 2, 2 * PASSES * P], U32, name="w_codes", align_bytes=64)
                w_scales = stream.tile([P, 2, 2 * PASSES * P], U8, name="w_scales", align_bytes=64)
                w_mx[rnd] = w_codes, w_scales
            w_codes, w_scales = w_mx[rnd]
            nc.vector.quantize_mx(out=w_codes[:, sides, :].rearrange("p s c -> p (s c)").bitcast(E5M2X4),
                                  scales=w_scales[:, sides, :].rearrange("p s c -> p (s c)"),
                                  in_=w_grouped[rnd][:, sides, :, :].rearrange("p s e c -> p (s e c)"))

        def multiply(step, side):
            w_codes, w_scales = w_mx[step // 2]
            if side == 0:
                waves[step] = psum.tile([P, B], F32, name="wave")
            for g in range(PASSES):
                first = ((step % 2) * PASSES + g) * P
                a = PASSES * side + g
                nc.tensor.matmul_mx(out=waves[step][:],
                                    lhsT=w_codes[:, side, first:first + P].bitcast(E5M2X4),
                                    lhsT_scale=w_scales[:, side, first:first + P],
                                    rhs=mov_codes[:, a, :].bitcast(E5M2X4), rhs_scale=mov_scales[:, a, :],
                                    start=(a == 0), stop=(a == 2 * PASSES - 1))

        def wave(gate, j):
            return waves[gate * TILES + j]

        def bias_of(gate, j):
            return bias[:, gate, j:j + 1]

        def act(out, in_, func, **affine):
            nc.scalar.activation(out=out, in_=in_, func=func, **affine)

        def stt(out, in0, scalar, op0, op1, in1):
            nc.vector.scalar_tensor_tensor(out=out, in0=in0, scalar=scalar, in1=in1, op0=op0, op1=op1)

        def tt(out, in0, op, in1):
            nc.vector.tensor_tensor(out=out, in0=in0, in1=in1, op=op)

        def do_n_plus_1(js):
            nc.gpsimd.tensor_scalar(out=n_plus_1[:, js, :], in0=n_sb[:, js, :], scalar1=1.0, scalar2=1.0,
                                    op0=ALU.add, op1=ALU.mult)

        def do_ln_n(js):
            act(ln_n[:, js, :], n_sb[:, js, :], ACT.Ln, bias=1.0)

        def do_inv_n(k):
            act(inv_n[:, pair(k), :], ln_n[:, pair(k), :], ACT.Exp, scale=-1.0)

        def do_abs_f(j):
            act(abs_f[:, j, :], wave(FORGET, j)[:], ACT.Abs, bias=bias_of(FORGET, j))

        def do_min_f(j):
            stt(min_f[:, j, :], wave(FORGET, j)[:], neg_bias_f[:, j:j + 1], ALU.min, ALU.add, m_sb[:, j, :])

        def do_exp_f(js):
            act(exp_f[:, js, :], abs_f[:, js, :], ACT.Exp, scale=-1.0)

        def do_ln_f(k):
            act(ln_f[:, pair(k), :], exp_f[:, pair(k), :], ACT.Ln, bias=1.0)

        def do_carry(j):
            stt(carry[:, j, :], min_f[:, j, :], bias_of(FORGET, j), ALU.add, ALU.subtract, ln_f[:, j, :])

        def do_gap_and_m(k):
            for j in (2 * k, 2 * k + 1):
                stt(gap[:, j, :], wave(INPUT, j)[:], bias_of(INPUT, j), ALU.add, ALU.subtract, carry[:, j, :])
                nc.gpsimd.tensor_scalar(out=gap[:, j, :], in0=gap[:, j, :], scalar1=GAP_LIMIT,
                                        scalar2=-GAP_LIMIT, op0=ALU.min, op1=ALU.max)
            for j in (2 * k, 2 * k + 1):
                stt(m_new[:, j, :], wave(INPUT, j)[:], bias_of(INPUT, j), ALU.add, ALU.max, carry[:, j, :])

        def do_exp_neg_gap(k):
            act(exp_neg_gap[:, pair(k), :], gap[:, pair(k), :], ACT.Exp, scale=-1.0)

        def do_exp_gap(k):
            act(exp_gap[:, pair(k), :], gap[:, pair(k), :], ACT.Exp)

        def do_n_new(k):
            stt(n_new[:, pair(k), :], exp_neg_gap[:, pair(k), :], 1.0, ALU.min, ALU.mult, n_plus_1[:, pair(k), :])
            store(out_n, n_new, pair(k))

        def do_tanh_z(k):
            tanh_z[k] = stream.tile([P, 2, B], F32, name="gate_value")
            for e in range(2):
                act(tanh_z[k][:, e, :], wave(Z, 2 * k + e)[:], ACT.Tanh, bias=bias_of(Z, 2 * k + e))

        def do_gained(k):
            tt(gained[:, pair(k), :], exp_gap[:, pair(k), :], ALU.mult, tanh_z[k][:])

        def do_inner(k):
            tt(inner[:, pair(k), :], gained[:, pair(k), :], ALU.add, c_sb[:, pair(k), :])

        def do_ratio(k):
            tt(ratio[:, pair(k), :], inv_n[:, pair(k), :], ALU.mult, inner[:, pair(k), :])

        def do_tanh_ratio(k):
            act(tanh_ratio[:, pair(k), :], ratio[:, pair(k), :], ACT.Tanh)

        def do_c_new(k):
            stt(c_new[:, pair(k), :], exp_neg_gap[:, pair(k), :], 1.0, ALU.min, ALU.mult, inner[:, pair(k), :])
            store(out_c, c_new, pair(k))

        def do_sigmoid_o(j, cols=slice(0, B)):
            if j // 2 not in sigmoid_o:
                sigmoid_o[j // 2] = stream.tile([P, 2, B], F32, name="gate_value")
            act(sigmoid_o[j // 2][:, j % 2, cols], wave(OUTPUT, j)[:, cols], ACT.Sigmoid, bias=bias_of(OUTPUT, j))

        def do_h_new(k):
            tt(h_new[:, pair(k), :], tanh_ratio[:, pair(k), :], ALU.mult, sigmoid_o[k][:])
            store(out_h, h_new, pair(k))

        def both(fn):
            return lambda k: (fn(2 * k), fn(2 * k + 1))

        on_scalar, on_vector = nc.scalar.copy, nc.vector.tensor_copy

        make_identity(nc, ident[:])
        load_state(n_sb, n_prev, tile(0))
        for a in range(2 * PASSES):
            load_moving(a)
            load_weights(0, a // 2, tile(a % 2))
        load_weight_tile(2)
        load_weight_tile(3)
        load_state(n_sb, n_prev, slice(1, TILES // 2))
        load_biases()
        load_weight_tile(4)
        load_state(n_sb, n_prev, slice(TILES // 2, TILES))
        load_state(m_sb, m_prev, pair(0))
        load_weight_tile(5)
        load_weight_tile(6)
        load_state(m_sb, m_prev, slice(2, TILES))
        load_weight_tile(7)
        for rnd in range(PAIRS, PRELOADED):
            load_weights(rnd, 0)
            load_weights(rnd, 1)

        do_ln_n(tile(0))
        for a in range(2 * PASSES):
            side, e = divmod(a, 2)
            group_moving(a, on_scalar, slice(0, SCALAR_COLS))
            group_moving(a, on_vector, slice(SCALAR_COLS, B))
            transpose_weights(e, side)
            empty_bank(e, side, on_scalar)
            quantise_moving(a)
            if e == 1:
                quantise_weights(0, slice(side, side + 1))
            if a == PASSES:
                multiply(0, 0)
                multiply(1, 0)
        for side in range(2):
            transpose_weights(LEAD - 1, side)
            empty_bank(LEAD - 1, side, on_vector)
        multiply(0, 1)
        multiply(1, 1)

        def at(first, fn, count=PAIRS):
            k, odd = divmod(step - first, 2)
            if not odd and 0 <= k < count:
                fn(k)

        last_f = TILES - 1
        for step in range(STEPS + 1):
            rnd, second = divmod(step, 2)
            if not second:
                if 0 < rnd <= ROUNDS - PRELOADED:
                    load_weights(PRELOADED + rnd - 1, 0)
                    load_weights(PRELOADED + rnd - 1, 1)
                if rnd == PAIRS - 1:
                    load_state(c_sb, c_prev, slice(0, TILES))
                for ahead in range(step + LEAD, min(step + LEAD + 2, STEPS)):
                    transpose_weights(ahead, 0)
                    transpose_weights(ahead, 1)
                if 0 < rnd < ROUNDS:
                    for s in (step, step + 1):
                        multiply(s, 0)
                        multiply(s, 1)

            if step == 1:
                nc.vector.tensor_copy(out=bias[:], in_=bias_raw[:, :, 0:TILES])
            at(READ, both(do_min_f), PAIRS - 1)
            at(Z * TILES + READ, do_tanh_z)
            at(NEW_H, both(do_sigmoid_o), PAIRS - 1)
            if step == 0:
                do_ln_n(slice(1, TILES // 2))
            if step == 1:
                do_ln_n(slice(TILES // 2, TILES))
            at(READ, both(do_abs_f), PAIRS - 1)
            if step == LOG_F:
                do_abs_f(last_f)
                do_min_f(last_f - 1)
                do_exp_f(tile(last_f))
                do_min_f(last_f)
                do_ln_f(0)
            if step == 0:
                for j in range(TILES):
                    do_n_plus_1(tile(j))
            at(GAP, do_gap_and_m)
            at(RATIO, do_ratio)
            at(INNER, do_gained)
            at(NEW_N, do_n_new)
            at(EXP_GAP, do_exp_neg_gap)
            if step + LEAD < STEPS:
                for side in range(2):
                    empty_bank(step + LEAD, side, on_vector if step in VECTOR_EMPTIES else on_scalar)
            if step == 1:
                nc.vector.tensor_scalar(out=neg_bias_f[:], in0=bias[:, FORGET, :], scalar1=-1.0, scalar2=None,
                                        op0=ALU.mult)
            if step in INV_N_STEPS:
                do_inv_n(INV_N_STEPS.index(step))
            at(READ + 1, lambda k: do_exp_f(pair(k)), PAIRS - 1)
            if step == LOG_F - 1:
                do_abs_f(last_f - 1)
                do_exp_f(tile(last_f - 1))
            if LOG_F < step < LOG_F + PAIRS:
                do_ln_f(step - LOG_F)
            at(EXP_GAP + 1, do_exp_gap)
            at(RATIO, do_tanh_ratio)
            at(INNER + 1, do_inner)
            if second and rnd + 1 < ROUNDS:
                quantise_weights(rnd + 1)
            at(CARRY, both(do_carry))
            at(RATIO, do_c_new)
            at(GAP + 1, lambda k: store(out_m, m_new, pair(k)))
            at(NEW_H, do_h_new, PAIRS - 1)

        for j, cols in ((TILES - 2, slice(0, B)), (TILES - 1, slice(0, B // 2)), (TILES - 1, slice(B // 2, B))):
            do_sigmoid_o(j, cols)
            tt(h_new[:, j, cols], tanh_ratio[:, j, cols], ALU.mult, sigmoid_o[j // 2][:, j % 2, cols])
            nc.sync.dma_start(out=out_h[:, j, cols], in_=h_new[:, j, cols])
